import numpy as np
import ml_dtypes


def mxq(x, axis, fmt="e4m3"):
    dtype, down = {"e4m3": (ml_dtypes.float8_e4m3fn, 7), "e5m2": (ml_dtypes.float8_e5m2, 14)}[fmt]
    v = np.moveaxis(np.asarray(x, np.float32).astype(ml_dtypes.bfloat16).astype(np.float64), axis, -1)
    blocks = v.reshape(v.shape[:-1] + (-1, 32))
    amax = np.abs(blocks).max(-1, keepdims=True)
    byte = np.maximum(np.where(amax > 0, np.frexp(amax)[1] - 1 + 127, 0) - down, 1)
    scale = np.exp2(byte - 127.0)
    codes = (blocks / scale).astype(np.float32).astype(dtype).astype(np.float64)
    return np.moveaxis((codes * scale).reshape(v.shape), -1, axis)


WIDE = False


def mx_kscale(k):
    if not WIDE:
        return np.ones(k)
    levels = np.array([10, -10, 5, -5, 0])
    if k % 512:
        return np.exp2(np.random.permutation(np.resize(levels, k // 32))).repeat(32)
    a = np.empty((k // 512, 16))
    for p in range(k // 512):
        a[p, :8] = np.random.permutation(np.resize(levels, 8))
        for g in range(8):
            far = levels[np.abs(levels - a[p, g]) >= 10]
            a[p, g + 8] = far[np.random.randint(len(far))]
    return np.exp2(a.ravel()).repeat(32)


BF16 = ml_dtypes.bfloat16


def bf(x):
    return np.asarray(x, np.float32).astype(BF16)


def f64(x):
    return np.asarray(x).astype(np.float64)


B, N, D, H, DH = 2, 2048, 4096, 64, 64
INNER = H * DH
S = 2 * DH


def dpfp(u):
    u2 = np.concatenate([np.maximum(u, 0.0), np.maximum(-u, 0.0)], axis=-1)
    return u2 * np.roll(u2, 1, axis=-1)


def setup_inputs():
    s, t = mx_kscale(D), mx_kscale(N)
    f = dpfp(np.random.standard_normal((B, H, N, DH)))
    return {"x": bf(np.random.standard_normal((B, N, D)) * s),
            "wv": bf(np.random.standard_normal((D, INNER)) / np.sqrt(D) / s[:, None]),
            "beta": bf(np.random.standard_normal((B, H, N)) * t),
            "vo": bf(np.random.standard_normal((B, H, N, DH)) * 0.3),
            "k_phi": bf(f / f.sum(-1, keepdims=True) / t[:, None]),
            "W": bf(np.random.standard_normal((B, H, S, DH)))}


def reference(x, wv, beta, vo, k_phi, W):
    v = mxq(f64(x), 2, "e4m3") @ mxq(f64(wv), 0, "e4m3")
    v = v.reshape(B, N, H, DH).transpose(0, 2, 1, 3)
    dv = f64(beta)[..., None] * (v - f64(vo))
    return f64(W) + (mxq(f64(k_phi).transpose(0, 1, 3, 2), 3, "e4m3") @ mxq(dv, 2, "e4m3"))

@@ -1,0 +1,455 @@
+from contextlib import ExitStack
+
+import concourse.mybir as mybir
+from concourse.masks import make_identity
+
+F32 = mybir.dt.float32
+BF16 = mybir.dt.bfloat16
+U32 = mybir.dt.uint32
+U8 = mybir.dt.uint8
+FP8X4 = mybir.dt.float8_e4m3fn_x4
+ALU = mybir.AluOpType
+ACT = mybir.ActivationFunctionType
+
+B, N, D, H, DH = 2, 2048, 4096, 64, 64
+S = 2 * DH
+FLOPS = 2 * B * N * D * H * DH + 2 * B * H * N * S * DH
+
+P = 128
+NB = 256
+HB = NB // DH
+NBLK = H * DH // NB
+NG = B * N // 512
+NPASS = D // 512
+NUNIT = NBLK * NG
+NHEAD = B * H
+LAG_K = 4
+LAG_S2 = 5
+NSLICE = NHEAD + LAG_S2 + 1
+KR_BUFS = 5
+
+
+def tile_dpfpattention_pb_l_kernel(tc, x, wv, beta, vo, k_phi, W, out):
+    nc = tc.nc
+    with ExitStack() as ctx:
+        keep = ctx.enter_context(tc.tile_pool(name="keep", bufs=1))
+        ring = ctx.enter_context(tc.tile_pool(name="ring", bufs=2))
+        psum = ctx.enter_context(tc.psum_pool(name="psum", bufs=1))
+        ctx.enter_context(tc.manual_schedule())
+
+        xview = x.flatten_outer_dims().rearrange("(g m t) k -> g m t k", m=P, t=4)
+
+        ident = keep.tile([P, P], F32, name="ident", tag="ident")
+        make_identity(nc, ident[:])
+        beta_t = keep.tile([P, 16, NHEAD], BF16, name="beta_t", tag="beta_t")
+
+        xc = {}
+        xs = {}
+        xraw = {}
+        xbank = {}
+        xgrp = {}
+        wraw = {}
+        wgrp = {}
+        wc = {}
+        ws = {}
+        kraw = {}
+        kgrp = {}
+        kc = {}
+        ks = {}
+        vt = {}
+        acc = {}
+        tmp = {}
+        dvg = {}
+        dvc = {}
+        dvs = {}
+        o2 = {}
+        wt = {}
+        bb = {}
+        braw = {}
+        xq = {"next": 0}
+
+        def x_tag(n):
+            G = n // 8
+            if G <= 5:
+                return "xc%d_%d" % (6 + (n % 8) // 4, n % 4)
+            if G == 6 and n % 2 == 0:
+                return "xc7_%d" % ((n // 2) % 4)
+            return "kr"
+
+        def x_load(n):
+            G, pi = n // 8, n % 8
+            tp, kq = pi // 4, pi % 4
+            tag = x_tag(n)
+            if tag == "kr":
+                t = ring.tile([P, 2, 1024], BF16, name="xr%d" % n, tag="kr", bufs=KR_BUFS)
+            else:
+                t = keep.tile([P, 2, 1024], BF16, name="xr%d" % n, tag=tag, align_bytes=64)
+            nc.sync.dma_start(out=t[:], in_=xview[G, :, 2 * tp : 2 * tp + 2, 1024 * kq : 1024 * (kq + 1)])
+            xraw[n] = t
+
+        def x_loads(done):
+            while xq["next"] < 64:
+                n = xq["next"]
+                tag = x_tag(n)
+                if n // 2 > done + 4:
+                    return
+                if tag == "kr":
+                    waiting = [m for m in range(2 * done + 2, n) if x_tag(m) == "kr"]
+                    if len(waiting) >= 3:
+                        return
+                elif xq.get(tag, -2) // 2 > done:
+                    return
+                x_load(n)
+                xq[tag] = n
+                xq["next"] = n + 1
+
+        def x_run(r):
+            for k in range(4):
+                n, gg = 2 * r + k // 2, k % 2
+                words = xraw[n][:].bitcast(F32)
+                bank = psum.tile([P, 512], F32, name="xb%d_%d" % (r, k), tag="ps", bufs=7)
+                for tt in range(2):
+                    for u in range(2):
+                        nc.tensor.transpose(
+                            bank[:, (2 * tt + u) * P : (2 * tt + u + 1) * P],
+                            words[:, tt, 256 * gg + u : 256 * (gg + 1) : 2],
+                            ident[:],
+                        )
+                xbank[(r, k)] = bank
+
+        def x_copy(r, k, eng):
+            g = ring.tile([P, 1024], BF16, name="xg%d_%d" % (r, k), tag="g2", bufs=10, align_bytes=64)
+            src = xbank.pop((r, k))[:].rearrange("p (tt u m) -> p tt m u", tt=2, u=2)
+            dst = g[:].bitcast(F32).rearrange("p (tt m u) -> p tt m u", tt=2, u=2)
+            if eng == "v":
+                nc.vector.tensor_copy(out=dst, in_=src)
+            else:
+                nc.scalar.copy(out=dst, in_=src)
+            xgrp[(r, k)] = g
+
+        def x_quant(r, k):
+            n, gg = 2 * r + k // 2, k % 2
+            G, pi = n // 8, n % 8
+            tp, kq = pi // 4, pi % 4
+            g = 2 * kq + gg
+            if (G, kq) not in xc:
+                xc[(G, kq)] = keep.tile([P, 2, 512], U32, name="xc%d_%d" % (G, kq), tag="xc%d_%d" % (G, kq), align_bytes=64)
+            if (G, g // 4) not in xs:
+                xs[(G, g // 4)] = keep.tile([P, 512], U8, name="xs%d_%d" % (G, g // 4), tag="xs%d_%d" % (G, g // 4), align_bytes=64)
+            cols = slice(256 * tp, 256 * (tp + 1))
+            nc.vector.quantize_mx(
+                out=xc[(G, kq)][:, gg, cols].bitcast(FP8X4),
+                scales=xs[(G, g // 4)][4 * (g % 4) : P, cols],
+                in_=xgrp.pop((r, k))[:],
+            )
+
+        def w_load(i):
+            if i >= NBLK * NPASS:
+                return
+            c, g = i // NPASS, i % NPASS
+            t = ring.tile([P, 4, NB], BF16, name="wr%d" % i, tag="wr", bufs=3)
+            nc.sync.dma_start(
+                out=t[:],
+                in_=wv[512 * g : 512 * (g + 1), NB * c : NB * (c + 1)].rearrange("(p j) w -> p j w", j=4),
+            )
+            wraw[i] = t
+
+        def w_il(i, eng):
+            if i >= NBLK * NPASS:
+                return
+            g = ring.tile([P, 1024], BF16, name="wg%d" % i, tag="g2", bufs=10, align_bytes=64)
+            src = wraw.pop(i)[:].rearrange("p j w -> p w j")
+            dst = g[:].rearrange("p (w j) -> p w j", j=4)
+            if eng == "v":
+                nc.vector.tensor_copy(out=dst, in_=src)
+            else:
+                nc.scalar.copy(out=dst, in_=src)
+            wgrp[i] = g
+
+        def w_quant(i):
+            if i >= NBLK * NPASS:
+                return
+            c, g = i // NPASS, i % NPASS
+            wc[i] = ring.tile([P, NB], U32, name="wc%d" % i, tag="wc%d" % g, bufs=2, align_bytes=64)
+            if g % 4 == 0:
+                ws[(c, g // 4)] = ring.tile([P, NB], U8, name="ws%d_%d" % (c, g // 4), tag="ws%d" % (g // 4), bufs=2, align_bytes=64)
+            nc.vector.quantize_mx(
+                out=wc[i][:].bitcast(FP8X4),
+                scales=ws[(c, g // 4)][4 * (g % 4) : P, :],
+                in_=wgrp.pop(i)[:],
+            )
+
+        def beta_load():
+            t = ring.tile([P, N], BF16, name="braw", tag="kr", bufs=KR_BUFS)
+            nc.sync.dma_start(out=t[:], in_=beta.rearrange("b h n -> (b h) n"))
+            braw[0] = t
+
+        def beta_turn(q):
+            bs = ring.tile([P, 512], F32, name="bs%d" % q, tag="tmp", bufs=3)
+            nc.vector.tensor_copy(
+                out=bs[:].rearrange("r (t p) -> r t p", t=4),
+                in_=braw[0][:, 512 * q : 512 * (q + 1)].rearrange("r (p t) -> r t p", t=4),
+            )
+            bank = psum.tile([P, 512], F32, name="bbk%d" % q, tag="ps", bufs=7)
+            for t in range(4):
+                nc.tensor.transpose(bank[:, P * t : P * (t + 1)], bs[:, P * t : P * (t + 1)], ident[:])
+            nc.scalar.copy(
+                out=beta_t[:, 4 * q : 4 * q + 4, :],
+                in_=bank[:].rearrange("p (t r) -> p t r", t=4),
+            )
+
+        def beta_block(c):
+            if c >= NBLK:
+                return
+            t = ring.tile([P, 16, B, HB], F32, name="bb%d" % c, tag="bb", bufs=2)
+            nc.gpsimd.tensor_copy(
+                out=t[:],
+                in_=beta_t[:].rearrange("p k (b h) -> p k b h", b=B)[:, :, :, HB * c : HB * (c + 1)],
+            )
+            bb[c] = t
+
+        def v_load(u):
+            if u >= NUNIT:
+                return
+            c, G = u // NG, u % NG
+            b, q = G // 4, G % 4
+            t = ring.tile([P, HB, 4 * DH], BF16, name="vt%d" % u, tag="vo", bufs=4)
+            nc.sync.dma_start(
+                out=t[:],
+                in_=vo[b, HB * c : HB * (c + 1), 512 * q : 512 * (q + 1), :].rearrange("h (p t) d -> p h (t d)", t=4),
+            )
+            vt[u] = t
+
+        def mm(u, t):
+            c, G = u // NG, u % NG
+            if t % 2 == 0:
+                acc[(u, t // 2)] = psum.tile([P, 512], F32, name="acc%d_%d" % (u, t // 2), tag="ps", bufs=7)
+            bank = acc[(u, t // 2)]
+            for g in range(NPASS):
+                nc.tensor.matmul_mx(
+                    out=bank[:, NB * (t % 2) : NB * (t % 2 + 1)],
+                    lhsT=xc[(G, g // 2)][:, g % 2, P * t : P * (t + 1)].bitcast(FP8X4),
+                    lhsT_scale=xs[(G, g // 4)][4 * (g % 4) : P, P * t : P * (t + 1)],
+                    rhs=wc[c * NPASS + g][:].bitcast(FP8X4),
+                    rhs_scale=ws[(c, g // 4)][4 * (g % 4) : P, :],
+                    start=(g == 0),
+                    stop=(g == NPASS - 1),
+                )
+
+        def sub(u, hf):
+            if u < 0 or u >= NUNIT:
+                return
+            d = ring.tile([P, 512], F32, name="tmp%d_%d" % (u, hf), tag="tmp", bufs=3)
+            nc.vector.tensor_tensor(
+                out=d[:].rearrange("p (t h d) -> p t h d", t=2, h=HB),
+                in0=acc.pop((u, hf))[:].rearrange("p (t h d) -> p t h d", t=2, h=HB),
+                in1=vt[u][:].rearrange("p h (t d) -> p t h d", t=4)[:, 2 * hf : 2 * hf + 2],
+                op=ALU.subtract,
+            )
+            tmp[(u, hf)] = d
+
+        def scale(u, hf):
+            if u < 0 or u >= NUNIT:
+                return
+            c, G = u // NG, u % NG
+            b, q = G // 4, G % 4
+            d = tmp.pop((u, hf))
+            for tl in range(2):
+                t = 2 * hf + tl
+                for h in range(HB):
+                    nc.scalar.activation(
+                        out=vt[u][:, h, DH * t : DH * (t + 1)],
+                        in_=d[:, (tl * HB + h) * DH : (tl * HB + h + 1) * DH],
+                        func=ACT.Copy,
+                        scale=bb[c][:, 4 * q + t, b, h : h + 1],
+                    )
+
+        def dv_il(u, eng):
+            if u < 0 or u >= NUNIT:
+                return
+            g = ring.tile([P, 1024], BF16, name="dvg%d" % u, tag="g2", bufs=10, align_bytes=64)
+            src = vt.pop(u)[:].rearrange("p h (t d) -> p h d t", t=4)
+            dst = g[:].rearrange("p (h d t) -> p h d t", h=HB, t=4)
+            if eng == "v":
+                nc.vector.tensor_copy(out=dst, in_=src)
+            else:
+                nc.scalar.copy(out=dst, in_=src)
+            dvg[u] = g
+
+        def dv_quant(u):
+            if u < 0 or u >= NUNIT:
+                return
+            q = u % 4
+            dvc[u] = ring.tile([P, NB], U32, name="dvc%d" % u, tag="dvc", bufs=8, align_bytes=64)
+            if q == 0:
+                dvs[u // 4] = ring.tile([P, NB], U8, name="dvs%d" % (u // 4), tag="dvs", bufs=2, align_bytes=64)
+            nc.vector.quantize_mx(
+                out=dvc[u][:].bitcast(FP8X4),
+                scales=dvs[u // 4][4 * q : P, :],
+                in_=dvg.pop(u)[:],
+            )
+
+        def head_of(i):
+            sg, hl = i // HB, i % HB
+            return sg % 2, HB * (sg // 2) + hl
+
+        def k_load(i):
+            if i < 0 or i >= NHEAD:
+                return
+            b, h = head_of(i)
+            t = ring.tile([P, 4, 512], BF16, name="kr%d" % i, tag="kr", bufs=KR_BUFS)
+            nc.sync.dma_start(out=t[:], in_=k_phi[b, h].rearrange("(q p t) s -> p q (t s)", q=4, t=4))
+            kraw[i] = t
+
+        def k_il(i, hf, eng):
+            if i < 0 or i >= NHEAD:
+                return
+            g = ring.tile([P, 1024], BF16, name="kg%d_%d" % (i, hf), tag="g2", bufs=10, align_bytes=64)
+            src = kraw[i][:, 2 * hf : 2 * hf + 2, :].rearrange("p q (t s) -> p q s t", t=4)
+            dst = g[:].rearrange("p (q s t) -> p q s t", q=2, t=4)
+            if eng == "v":
+                nc.vector.tensor_copy(out=dst, in_=src)
+            else:
+                nc.scalar.copy(out=dst, in_=src)
+            kgrp[(i, hf)] = g
+
+        def k_quant(i, hf):
+            if i < 0 or i >= NHEAD:
+                return
+            if hf == 0:
+                kc[i] = ring.tile([P, 512], U32, name="kc%d" % i, tag="kc", bufs=3, align_bytes=64)
+                ks[i] = ring.tile([P, 512], U8, name="ks%d" % i, tag="ks", bufs=3, align_bytes=64)
+            cols = slice(256 * hf, 256 * (hf + 1))
+            nc.vector.quantize_mx(
+                out=kc[i][:, cols].bitcast(FP8X4),
+                scales=ks[i][:, cols],
+                in_=kgrp.pop((i, hf))[:],
+            )
+
+        def s2(i):
+            if i < 0 or i >= NHEAD:
+                return
+            sg, hl = i // HB, i % HB
+            if hl == 0:
+                o2[sg] = psum.tile([P, 512], F32, name="o2_%d" % sg, tag="o2", bufs=1)
+            cols = slice(P * (hl // 2), P * (hl // 2 + 1))
+            for q in range(4):
+                nc.tensor.matmul_mx(
+                    out=o2[sg][:, P * hl : P * (hl + 1)],
+                    lhsT=kc[i][:, P * q : P * (q + 1)].bitcast(FP8X4),
+                    lhsT_scale=ks[i][:, P * q : P * (q + 1)],
+                    rhs=dvc[4 * sg + q][:, cols].bitcast(FP8X4),
+                    rhs_scale=dvs[sg][4 * q : P, cols],
+                    start=(q == 0),
+                    stop=(q == 3),
+                )
+
+        def out_view(ap, sg):
+            b, c = sg % 2, sg // 2
+            return ap[b, HB * c : HB * (c + 1)].rearrange("h s d -> s h d")
+
+        def big_w_load(sg):
+            if sg < 0 or sg >= 2 * NBLK:
+                return
+            t = ring.tile([P, HB, DH], BF16, name="wt%d" % sg, tag="wt", bufs=2)
+            nc.sync.dma_start(out=t[:], in_=out_view(W, sg))
+            wt[sg] = t
+
+        def evac(sg):
+            o = ring.tile([P, HB, DH], F32, name="osb%d" % sg, tag="osb", bufs=2)
+            nc.vector.tensor_tensor(
+                out=o[:].rearrange("p (j e) d -> p j e d", e=2),
+                in0=o2.pop(sg)[:].rearrange("p (j z d) -> p j z d", j=2, z=4)[:, :, 0:4:3, :],
+                in1=wt.pop(sg)[:].rearrange("p (j e) d -> p j e d", e=2),
+                op=ALU.add,
+            )
+            nc.sync.dma_start(out=out_view(out, sg), in_=o[:])
+
+        for n in (0, 1):
+            x_load(n)
+        w_load(0)
+        w_load(1)
+        x_load(2)
+        x_load(3)
+        w_load(2)
+        x_load(4)
+        x_load(5)
+        for n in range(6):
+            xq[x_tag(n)] = n
+        xq["next"] = 6
+        for r in range(4):
+            x_run(r)
+            if r > 0:
+                for k in range(4):
+                    x_quant(r - 1, k)
+            x_copy(r, 0, "v")
+            for k in range(1, 4):
+                x_copy(r, k, "s")
+            w_il(2 * r, "v")
+            w_il(2 * r + 1, "s")
+            if r > 0:
+                w_quant(2 * r - 2)
+                w_quant(2 * r - 1)
+            w_load(2 * r + 3)
+            w_load(2 * r + 4)
+            x_loads(r - 1)
+        beta_load()
+        v_load(0)
+        v_load(1)
+        w_quant(6)
+        w_quant(7)
+        w_il(8, "s")
+
+        for u in range(NSLICE):
+            head_a = u < NG - 1
+            v_load(u + 2)
+            w_load(u + 11)
+            if u >= NG:
+                k_load(u + 2 - LAG_K)
+            if u == NG:
+                k_load(u + 1 - LAG_K)
+            if u < NG:
+                k_load(u + 1 - LAG_K)
+            if u % 4 == 2:
+                big_w_load((u - 6) // 4)
+            if u % NG == 4:
+                beta_block(u // NG + 1)
+            for j in range(4):
+                r = 4 * (u + 1) + j
+                if j == 2:
+                    s2(u - LAG_S2)
+                if u < NUNIT:
+                    mm(u, j)
+                if head_a:
+                    x_run(r)
+                    x_loads(r)
+                if u == 0 and j < 2:
+                    beta_turn(2 * j)
+                    beta_turn(2 * j + 1)
+                    if j == 1:
+                        beta_block(0)
+                if j == 0:
+                    sub(u - 1, 1)
+                    k_il(u - LAG_K, 0, "v")
+                    scale(u - 1, 1)
+                elif j == 1:
+                    w_quant(u + 8)
+                    k_il(u - LAG_K, 1, "v")
+                    dv_il(u - 1, "s")
+                elif j == 2:
+                    sub(u, 0)
+                    k_quant(u - LAG_K, 0)
+                    dv_quant(u - 1)
+                    scale(u, 0)
+                else:
+                    k_quant(u - LAG_K, 1)
+                    if u >= 8 and u % 4 == 0:
+                        evac((u - 8) // 4)
+                    w_il(u + 9, "s")
+                if u < NG and r - 1 < 32:
+                    for k in range(4):
+                        x_quant(r - 1, k)
+                if head_a:
+                    x_copy(r, 0, "v")
+                    for k in range(1, 4):
+                        x_copy(r, k, "s")

@@ -27,6 +27,8 @@ LAG_K = 4
 LAG_S2 = 5
 NSLICE = NHEAD + LAG_S2 + 1
 KR_BUFS = 5
+EARLY = NHEAD - HB
+LATE0 = NUNIT - 9
 
 
 def tile_dpfpattention_pb_l_kernel(tc, x, wv, beta, vo, k_phi, W, out):
@@ -66,7 +68,8 @@ def tile_dpfpattention_pb_l_kernel(tc, x, wv, beta, vo, k_phi, W, out):
         wt = {}
         bb = {}
         braw = {}
-        xq = {"next": 0}
+        kdone = {}
+        xq = {"next": 0, "quantised": -1}
 
         def x_tag(n):
             G = n // 8
@@ -127,6 +130,20 @@ def tile_dpfpattention_pb_l_kernel(tc, x, wv, beta, vo, k_phi, W, out):
                 nc.scalar.copy(out=dst, in_=src)
             xgrp[(r, k)] = g
 
+        def x_need(run):
+            while xq["quantised"] < run:
+                xq["quantised"] += 1
+                for k in range(4):
+                    x_quant(xq["quantised"], k)
+
+        def x_turn(r):
+            x_run(r)
+            x_loads(r)
+            x_need(r - 1)
+            x_copy(r, 0, "v")
+            for k in range(1, 4):
+                x_copy(r, k, "s")
+
         def x_quant(r, k):
             n, gg = 2 * r + k // 2, k % 2
             G, pi = n // 8, n % 8
@@ -147,7 +164,10 @@ def tile_dpfpattention_pb_l_kernel(tc, x, wv, beta, vo, k_phi, W, out):
             if i >= NBLK * NPASS:
                 return
             c, g = i // NPASS, i % NPASS
-            t = ring.tile([P, 4, NB], BF16, name="wr%d" % i, tag="wr", bufs=3)
+            if 3 <= i <= 6:
+                t = ring.tile([P, 4, NB], BF16, name="wr%d" % i, tag="vo", bufs=4)
+            else:
+                t = ring.tile([P, 4, NB], BF16, name="wr%d" % i, tag="wr", bufs=3, align_bytes=64)
             nc.sync.dma_start(
                 out=t[:],
                 in_=wv[512 * g : 512 * (g + 1), NB * c : NB * (c + 1)].rearrange("(p j) w -> p j w", j=4),
@@ -222,6 +242,8 @@ def tile_dpfpattention_pb_l_kernel(tc, x, wv, beta, vo, k_phi, W, out):
 
         def mm(u, t):
             c, G = u // NG, u % NG
+            if c == 0:
+                x_need(4 * G + 1 + 2 * (t // 2))
             if t % 2 == 0:
                 acc[(u, t // 2)] = psum.tile([P, 512], F32, name="acc%d_%d" % (u, t // 2), tag="ps", bufs=7)
             bank = acc[(u, t // 2)]
@@ -302,8 +324,9 @@ def tile_dpfpattention_pb_l_kernel(tc, x, wv, beta, vo, k_phi, W, out):
             kraw[i] = t
 
         def k_il(i, hf, eng):
-            if i < 0 or i >= NHEAD:
+            if i < 0 or i >= NHEAD or (i, hf) in kdone:
                 return
+            kdone[(i, hf)] = 1
             g = ring.tile([P, 1024], BF16, name="kg%d_%d" % (i, hf), tag="g2", bufs=10, align_bytes=64)
             src = kraw[i][:, 2 * hf : 2 * hf + 2, :].rearrange("p q (t s) -> p q s t", t=4)
             dst = g[:].rearrange("p (q s t) -> p q s t", q=2, t=4)
@@ -314,11 +337,19 @@ def tile_dpfpattention_pb_l_kernel(tc, x, wv, beta, vo, k_phi, W, out):
             kgrp[(i, hf)] = g
 
         def k_quant(i, hf):
-            if i < 0 or i >= NHEAD:
+            if i < 0 or i >= NHEAD or (i, hf) not in kgrp:
                 return
-            if hf == 0:
+            if hf == 0 and i < EARLY:
                 kc[i] = ring.tile([P, 512], U32, name="kc%d" % i, tag="kc", bufs=3, align_bytes=64)
                 ks[i] = ring.tile([P, 512], U8, name="ks%d" % i, tag="ks", bufs=3, align_bytes=64)
+            elif hf == 0:
+                if i == EARLY:
+                    ks["late"] = ring.tile([P, HB, 512], U8, name="kslate", tag="g2", bufs=10, align_bytes=64)
+                if i < NHEAD - 1:
+                    kc[i] = ring.tile([P, 512], U32, name="kc%d" % i, tag="wr", bufs=3, align_bytes=64)
+                else:
+                    kc[i] = ring.tile([P, 512], U32, name="kc%d" % i, tag="g2", bufs=10, align_bytes=64)
+                ks[i] = ks["late"][:, i - EARLY, :]
             cols = slice(256 * hf, 256 * (hf + 1))
             nc.vector.quantize_mx(
                 out=kc[i][:, cols].bitcast(FP8X4),
@@ -330,8 +361,10 @@ def tile_dpfpattention_pb_l_kernel(tc, x, wv, beta, vo, k_phi, W, out):
             if i < 0 or i >= NHEAD:
                 return
             sg, hl = i // HB, i % HB
-            if hl == 0:
+            if hl == 0 and i < EARLY:
                 o2[sg] = psum.tile([P, 512], F32, name="o2_%d" % sg, tag="o2", bufs=1)
+            elif hl == 0:
+                o2[sg] = psum.tile([P, 512], F32, name="o2_%d" % sg, tag="ps", bufs=7)
             cols = slice(P * (hl // 2), P * (hl // 2 + 1))
             for q in range(4):
                 nc.tensor.matmul_mx(
@@ -365,91 +398,111 @@ def tile_dpfpattention_pb_l_kernel(tc, x, wv, beta, vo, k_phi, W, out):
             )
             nc.sync.dma_start(out=out_view(out, sg), in_=o[:])
 
-        for n in (0, 1):
-            x_load(n)
-        w_load(0)
-        w_load(1)
+        x_load(0)
+        x_load(1)
+        beta_load()
         x_load(2)
         x_load(3)
-        w_load(2)
+        for i in range(4):
+            w_load(i)
         x_load(4)
         x_load(5)
+        for i in range(4, 7):
+            w_load(i)
         for n in range(6):
             xq[x_tag(n)] = n
         xq["next"] = 6
-        for r in range(4):
-            x_run(r)
-            if r > 0:
-                for k in range(4):
-                    x_quant(r - 1, k)
-            x_copy(r, 0, "v")
-            for k in range(1, 4):
-                x_copy(r, k, "s")
-            w_il(2 * r, "v")
-            w_il(2 * r + 1, "s")
-            if r > 0:
-                w_quant(2 * r - 2)
-                w_quant(2 * r - 1)
-            w_load(2 * r + 3)
-            w_load(2 * r + 4)
-            x_loads(r - 1)
-        beta_load()
+        x_run(0)
+        x_copy(0, 0, "v")
+        for k in range(1, 4):
+            x_copy(0, k, "s")
+        for q in range(4):
+            beta_turn(q)
+        beta_block(0)
+        x_need(0)
+        x_run(1)
+        x_copy(1, 0, "v")
+        for k in range(1, 4):
+            x_copy(1, k, "s")
+        w_il(0, "v")
+        w_load(7)
+        x_loads(1)
+        w_il(1, "v")
+        w_il(2, "s")
+        x_need(1)
+        w_quant(0)
+        w_quant(1)
+        w_il(3, "v")
+        w_quant(2)
+        x_turn(2)
+        w_il(4, "v")
+        w_il(5, "s")
+        w_quant(3)
+        w_quant(4)
+        w_il(6, "v")
+        w_quant(5)
+        w_il(7, "v")
+        w_quant(6)
+        w_load(8)
+        w_load(9)
         v_load(0)
         v_load(1)
-        w_quant(6)
         w_quant(7)
-        w_il(8, "s")
 
         for u in range(NSLICE):
-            head_a = u < NG - 1
             v_load(u + 2)
-            w_load(u + 11)
-            if u >= NG:
+            if u < 2:
+                w_load(u + 10)
+            if u > 0:
+                w_load(u + 11)
+            if u >= NG and u + 2 - LAG_K < EARLY:
                 k_load(u + 2 - LAG_K)
             if u == NG:
                 k_load(u + 1 - LAG_K)
             if u < NG:
                 k_load(u + 1 - LAG_K)
+            if u >= LATE0 - 2 and (u - LATE0) % 2 == 0:
+                k_load(EARLY + (u - LATE0 + 2) // 2)
             if u % 4 == 2:
-                big_w_load((u - 6) // 4)
+                big_w_load((u - 2) // 4)
             if u % NG == 4:
                 beta_block(u // NG + 1)
             for j in range(4):
-                r = 4 * (u + 1) + j
-                if j == 2:
+                if j == 2 and u < NUNIT:
+                    s2(u - LAG_S2)
+                if j == 0 and u >= NUNIT:
                     s2(u - LAG_S2)
                 if u < NUNIT:
                     mm(u, j)
-                if head_a:
-                    x_run(r)
-                    x_loads(r)
-                if u == 0 and j < 2:
-                    beta_turn(2 * j)
-                    beta_turn(2 * j + 1)
-                    if j == 1:
-                        beta_block(0)
+                r = 4 * u + j + 3
+                if r < 32:
+                    x_turn(r)
                 if j == 0:
                     sub(u - 1, 1)
+                    if u == NUNIT:
+                        evac(2 * NBLK - 2)
                     k_il(u - LAG_K, 0, "v")
                     scale(u - 1, 1)
                 elif j == 1:
-                    w_quant(u + 8)
+                    if u > 0:
+                        w_quant(u + 8)
+                    if LATE0 < u <= LATE0 + 8:
+                        k_quant(EARLY + (u - LATE0 - 1) // 2, (u - LATE0 - 1) % 2)
                     k_il(u - LAG_K, 1, "v")
-                    dv_il(u - 1, "s")
+                    dv_il(u - 1, "s" if u < NUNIT else "v")
                 elif j == 2:
                     sub(u, 0)
                     k_quant(u - LAG_K, 0)
                     dv_quant(u - 1)
                     scale(u, 0)
+                    if u == 0:
+                        w_il(8, "s")
                 else:
+                    if u == 0:
+                        w_quant(8)
                     k_quant(u - LAG_K, 1)
-                    if u >= 8 and u % 4 == 0:
+                    if u >= 8 and u % 4 == 0 and u != NUNIT:
                         evac((u - 8) // 4)
                     w_il(u + 9, "s")
-                if u < NG and r - 1 < 32:
-                    for k in range(4):
-                        x_quant(r - 1, k)
-                if head_a:
-                    x_copy(r, 0, "v")
-                    for k in range(1, 4):
-                        x_copy(r, k, "s")
+                    if LATE0 <= u < LATE0 + 8:
+                        k_il(EARLY + (u - LATE0) // 2, (u - LATE0) % 2, "s")

@@ -29,6 +29,7 @@ NSLICE = NHEAD + LAG_S2 + 1
 KR_BUFS = 5
 EARLY = NHEAD - HB
 LATE0 = NUNIT - 9
+DV_IL = ("v", "v")
 
 
 def tile_dpfpattention_pb_l_kernel(tc, x, wv, beta, vo, k_phi, W, out):
@@ -258,10 +259,21 @@ def tile_dpfpattention_pb_l_kernel(tc, x, wv, beta, vo, k_phi, W, out):
                     stop=(g == NPASS - 1),
                 )
 
+        def lift(u, hf):
+            if u < 0 or u >= NUNIT - 1:
+                return
+            d = ring.tile([P, 512], F32, name="tmp%d_%d" % (u, hf), tag="tmp", bufs=3)
+            nc.scalar.copy(out=d[:], in_=acc.pop((u, hf))[:])
+            acc[(u, hf)] = d
+            tmp[(u, hf)] = d
+
         def sub(u, hf):
             if u < 0 or u >= NUNIT:
                 return
-            d = ring.tile([P, 512], F32, name="tmp%d_%d" % (u, hf), tag="tmp", bufs=3)
+            if (u, hf) in tmp:
+                d = tmp[(u, hf)]
+            else:
+                d = ring.tile([P, 512], F32, name="tmp%d_%d" % (u, hf), tag="tmp", bufs=3)
             nc.vector.tensor_tensor(
                 out=d[:].rearrange("p (t h d) -> p t h d", t=2, h=HB),
                 in0=acc.pop((u, hf))[:].rearrange("p (t h d) -> p t h d", t=2, h=HB),
@@ -478,31 +490,34 @@ def tile_dpfpattention_pb_l_kernel(tc, x, wv, beta, vo, k_phi, W, out):
                 if r < 32:
                     x_turn(r)
                 if j == 0:
-                    sub(u - 1, 1)
+                    lift(u - 1, 1)
+                    if u > 0:
+                        w_il(u + 9, "s")
                     if u == NUNIT:
                         evac(2 * NBLK - 2)
                     k_il(u - LAG_K, 0, "v")
-                    scale(u - 1, 1)
+                    sub(u - 1, 1)
                 elif j == 1:
                     if u > 0:
                         w_quant(u + 8)
                     if LATE0 < u <= LATE0 + 8:
                         k_quant(EARLY + (u - LATE0 - 1) // 2, (u - LATE0 - 1) % 2)
                     k_il(u - LAG_K, 1, "v")
-                    dv_il(u - 1, "s" if u < NUNIT else "v")
+                    scale(u - 1, 1)
                 elif j == 2:
                     sub(u, 0)
                     k_quant(u - LAG_K, 0)
-                    dv_quant(u - 1)
                     scale(u, 0)
+                    dv_il(u - 1, DV_IL[u % 2] if u < NUNIT else "v")
                     if u == 0:
                         w_il(8, "s")
                 else:
                     if u == 0:
                         w_quant(8)
+                        w_il(9, "s")
                     k_quant(u - LAG_K, 1)
+                    dv_quant(u - 1)
                     if u >= 8 and u % 4 == 0 and u != NUNIT:
                         evac((u - 8) // 4)
-                    w_il(u + 9, "s")
                     if LATE0 <= u < LATE0 + 8:
                         k_il(EARLY + (u - LATE0) // 2, (u - LATE0) % 2, "s")

@@ -16,20 +16,37 @@ S = 2 * DH
 FLOPS = 2 * B * N * D * H * DH + 2 * B * H * N * S * DH
 
 P = 128
-NB = 256
-HB = NB // DH
-NBLK = H * DH // NB
-NG = B * N // 512
-NPASS = D // 512
-NUNIT = NBLK * NG
-NHEAD = B * H
-LAG_K = 4
-LAG_S2 = 5
-NSLICE = NHEAD + LAG_S2 + 1
-KR_BUFS = 5
-EARLY = NHEAD - HB
-LATE0 = NUNIT - 9
-DV_IL = ("v", "v")
+PACK = 4
+K_PASS = P * PACK
+COLS = 256
+HEADS = COLS // DH
+N_BLOCKS = H * DH // COLS
+N_GROUPS = B * N // K_PASS
+GROUPS_PER_BATCH = N // K_PASS
+N_PASSES = D // K_PASS
+N_UNITS = N_BLOCKS * N_GROUPS
+N_SETS = B * N_BLOCKS
+N_HEADS = B * H
+N_W = N_BLOCKS * N_PASSES
+N_PIECES = 8 * N_GROUPS
+N_RUNS = N_PIECES // 2
+QUANT = 1024
+
+S2_LAG = 5
+KEY_LAG = 4
+N_SLICES = N_HEADS + S2_LAG + 1
+RUN_LEAD = 3
+LAST_SET = N_HEADS - HEADS
+IDLE_W = N_UNITS - 9
+
+KEY_BUFS = 5
+W_BUFS = 3
+VO_BUFS = 4
+STAGE_BUFS = 10
+DIFF_BUFS = 3
+DV_BUFS = 8
+CODE_BUFS = 3
+BANKS = 7
 
 
 def tile_dpfpattention_pb_l_kernel(tc, x, wv, beta, vo, k_phi, W, out):
@@ -40,375 +57,354 @@ def tile_dpfpattention_pb_l_kernel(tc, x, wv, beta, vo, k_phi, W, out):
         psum = ctx.enter_context(tc.psum_pool(name="psum", bufs=1))
         ctx.enter_context(tc.manual_schedule())
 
-        xview = x.flatten_outer_dims().rearrange("(g m t) k -> g m t k", m=P, t=4)
+        x_view = x.flatten_outer_dims().rearrange("(g m t) k -> g m t k", m=P, t=PACK)
 
         ident = keep.tile([P, P], F32, name="ident", tag="ident")
         make_identity(nc, ident[:])
-        beta_t = keep.tile([P, 16, NHEAD], BF16, name="beta_t", tag="beta_t")
+        beta_t = keep.tile([P, PACK * GROUPS_PER_BATCH, N_HEADS], BF16, name="beta_t", tag="beta_t")
 
-        xc = {}
-        xs = {}
-        xraw = {}
-        xbank = {}
-        xgrp = {}
-        wraw = {}
-        wgrp = {}
-        wc = {}
-        ws = {}
-        kraw = {}
-        kgrp = {}
-        kc = {}
-        ks = {}
-        vt = {}
-        acc = {}
-        tmp = {}
-        dvg = {}
-        dvc = {}
-        dvs = {}
-        o2 = {}
-        wt = {}
-        bb = {}
-        braw = {}
-        kdone = {}
-        xq = {"next": 0, "quantised": -1}
+        x_raw, x_bank, x_stage, x_codes, x_planes = {}, {}, {}, {}, {}
+        w_raw, w_stage, w_codes, w_planes = {}, {}, {}, {}
+        key_raw, key_stage, key_codes, key_planes = {}, {}, {}, {}
+        vo_dv, v_bank, diff, dv_stage, dv_codes, dv_planes = {}, {}, {}, {}, {}, {}
+        beta_raw, beta_cols, sums, w_mem = {}, {}, {}, {}
+        x_state = {"next piece": 0, "quantised run": -1}
 
-        def x_tag(n):
-            G = n // 8
-            if G <= 5:
+        def copy_on(engine, dst, src):
+            if engine == "vector":
+                nc.vector.tensor_copy(out=dst, in_=src)
+            else:
+                nc.scalar.copy(out=dst, in_=src)
+
+        def stage_tile(name):
+            return ring.tile([P, QUANT], BF16, name=name, tag="g2", bufs=STAGE_BUFS, align_bytes=64)
+
+
+        def x_raw_tag(n):
+            group = n // 8
+            if group <= 5:
                 return "xc%d_%d" % (6 + (n % 8) // 4, n % 4)
-            if G == 6 and n % 2 == 0:
+            if group == 6 and n % 2 == 0:
                 return "xc7_%d" % ((n // 2) % 4)
             return "kr"
 
         def x_load(n):
-            G, pi = n // 8, n % 8
-            tp, kq = pi // 4, pi % 4
-            tag = x_tag(n)
+            group, tp, kq = n // 8, (n % 8) // 4, n % 4
+            tag = x_raw_tag(n)
             if tag == "kr":
-                t = ring.tile([P, 2, 1024], BF16, name="xr%d" % n, tag="kr", bufs=KR_BUFS)
+                t = ring.tile([P, 2, 1024], BF16, name="xr%d" % n, tag="kr", bufs=KEY_BUFS)
             else:
                 t = keep.tile([P, 2, 1024], BF16, name="xr%d" % n, tag=tag, align_bytes=64)
-            nc.sync.dma_start(out=t[:], in_=xview[G, :, 2 * tp : 2 * tp + 2, 1024 * kq : 1024 * (kq + 1)])
-            xraw[n] = t
+            nc.sync.dma_start(out=t[:], in_=x_view[group, :, 2 * tp : 2 * tp + 2, 1024 * kq : 1024 * (kq + 1)])
+            x_raw[n] = t
+            x_state[tag] = n
+            x_state["next piece"] = n + 1
 
-        def x_loads(done):
-            while xq["next"] < 64:
-                n = xq["next"]
-                tag = x_tag(n)
-                if n // 2 > done + 4:
+        def x_load_ahead(turned):
+            while x_state["next piece"] < N_PIECES:
+                n = x_state["next piece"]
+                tag = x_raw_tag(n)
+                if n // 2 > turned + 4:
                     return
                 if tag == "kr":
-                    waiting = [m for m in range(2 * done + 2, n) if x_tag(m) == "kr"]
-                    if len(waiting) >= 3:
+                    if len([m for m in range(2 * turned + 2, n) if x_raw_tag(m) == "kr"]) >= 3:
                         return
-                elif xq.get(tag, -2) // 2 > done:
+                elif x_state.get(tag, -2) // 2 > turned:
                     return
                 x_load(n)
-                xq[tag] = n
-                xq["next"] = n + 1
 
-        def x_run(r):
-            for k in range(4):
-                n, gg = 2 * r + k // 2, k % 2
-                words = xraw[n][:].bitcast(F32)
-                bank = psum.tile([P, 512], F32, name="xb%d_%d" % (r, k), tag="ps", bufs=7)
+        def x_transpose(r, half):
+            for i in (2 * half, 2 * half + 1):
+                words = x_raw[2 * r + i // 2][:].bitcast(F32)
+                first = 256 * (i % 2)
+                bank = psum.tile([P, 512], F32, name="xb%d_%d" % (r, i), tag="ps", bufs=BANKS)
                 for tt in range(2):
                     for u in range(2):
                         nc.tensor.transpose(
                             bank[:, (2 * tt + u) * P : (2 * tt + u + 1) * P],
-                            words[:, tt, 256 * gg + u : 256 * (gg + 1) : 2],
+                            words[:, tt, first + u : first + 256 : 2],
                             ident[:],
                         )
-                xbank[(r, k)] = bank
+                x_bank[(r, i)] = bank
 
-        def x_copy(r, k, eng):
-            g = ring.tile([P, 1024], BF16, name="xg%d_%d" % (r, k), tag="g2", bufs=10, align_bytes=64)
-            src = xbank.pop((r, k))[:].rearrange("p (tt u m) -> p tt m u", tt=2, u=2)
-            dst = g[:].bitcast(F32).rearrange("p (tt m u) -> p tt m u", tt=2, u=2)
-            if eng == "v":
-                nc.vector.tensor_copy(out=dst, in_=src)
-            else:
-                nc.scalar.copy(out=dst, in_=src)
-            xgrp[(r, k)] = g
+        def x_copy(r, i, engine):
+            t = stage_tile("xg%d_%d" % (r, i))
+            copy_on(
+                engine,
+                t[:].bitcast(F32).rearrange("p (tt m u) -> p tt m u", tt=2, u=2),
+                x_bank.pop((r, i))[:].rearrange("p (tt u m) -> p tt m u", tt=2, u=2),
+            )
+            x_stage[(r, i)] = t
 
-        def x_need(run):
-            while xq["quantised"] < run:
-                xq["quantised"] += 1
-                for k in range(4):
-                    x_quant(xq["quantised"], k)
-
-        def x_turn(r):
-            x_run(r)
-            x_loads(r)
-            x_need(r - 1)
-            x_copy(r, 0, "v")
-            for k in range(1, 4):
-                x_copy(r, k, "s")
-
-        def x_quant(r, k):
-            n, gg = 2 * r + k // 2, k % 2
-            G, pi = n // 8, n % 8
-            tp, kq = pi // 4, pi % 4
-            g = 2 * kq + gg
-            if (G, kq) not in xc:
-                xc[(G, kq)] = keep.tile([P, 2, 512], U32, name="xc%d_%d" % (G, kq), tag="xc%d_%d" % (G, kq), align_bytes=64)
-            if (G, g // 4) not in xs:
-                xs[(G, g // 4)] = keep.tile([P, 512], U8, name="xs%d_%d" % (G, g // 4), tag="xs%d_%d" % (G, g // 4), align_bytes=64)
+        def x_quantize(r, i):
+            n = 2 * r + i // 2
+            group, tp, kq = n // 8, (n % 8) // 4, n % 4
+            g = 2 * kq + i % 2
+            if (group, kq) not in x_codes:
+                x_codes[(group, kq)] = keep.tile(
+                    [P, 2, K_PASS], U32, name="xc%d_%d" % (group, kq), tag="xc%d_%d" % (group, kq), align_bytes=64
+                )
+            if (group, g // 4) not in x_planes:
+                x_planes[(group, g // 4)] = keep.tile(
+                    [P, K_PASS], U8, name="xs%d_%d" % (group, g // 4), tag="xs%d_%d" % (group, g // 4), align_bytes=64
+                )
             cols = slice(256 * tp, 256 * (tp + 1))
             nc.vector.quantize_mx(
-                out=xc[(G, kq)][:, gg, cols].bitcast(FP8X4),
-                scales=xs[(G, g // 4)][4 * (g % 4) : P, cols],
-                in_=xgrp.pop((r, k))[:],
+                out=x_codes[(group, kq)][:, g % 2, cols].bitcast(FP8X4),
+                scales=x_planes[(group, g // 4)][4 * (g % 4) : P, cols],
+                in_=x_stage.pop((r, i))[:],
             )
+
+        def x_quantize_through(r):
+            while x_state["quantised run"] < r:
+                x_state["quantised run"] += 1
+                for i in range(4):
+                    x_quantize(x_state["quantised run"], i)
+
+        def x_half_run(r, half):
+            x_transpose(r, half)
+            if half == 0:
+                x_quantize_through(r - 1)
+                x_copy(r, 0, "vector")
+                x_copy(r, 1, "scalar")
+            else:
+                x_copy(r, 2, "scalar")
+                x_copy(r, 3, "scalar")
+
 
         def w_load(i):
-            if i >= NBLK * NPASS:
+            if i >= N_W:
                 return
-            c, g = i // NPASS, i % NPASS
+            block, g = i // N_PASSES, i % N_PASSES
             if 3 <= i <= 6:
-                t = ring.tile([P, 4, NB], BF16, name="wr%d" % i, tag="vo", bufs=4)
+                t = ring.tile([P, PACK, COLS], BF16, name="wr%d" % i, tag="vo", bufs=VO_BUFS)
             else:
-                t = ring.tile([P, 4, NB], BF16, name="wr%d" % i, tag="wr", bufs=3, align_bytes=64)
+                t = ring.tile([P, PACK, COLS], BF16, name="wr%d" % i, tag="wr", bufs=W_BUFS, align_bytes=64)
             nc.sync.dma_start(
                 out=t[:],
-                in_=wv[512 * g : 512 * (g + 1), NB * c : NB * (c + 1)].rearrange("(p j) w -> p j w", j=4),
+                in_=wv[K_PASS * g : K_PASS * (g + 1), COLS * block : COLS * (block + 1)].rearrange(
+                    "(p j) w -> p j w", j=PACK
+                ),
             )
-            wraw[i] = t
+            w_raw[i] = t
 
-        def w_il(i, eng):
-            if i >= NBLK * NPASS:
+        def w_interleave(i, engine):
+            if i >= N_W:
                 return
-            g = ring.tile([P, 1024], BF16, name="wg%d" % i, tag="g2", bufs=10, align_bytes=64)
-            src = wraw.pop(i)[:].rearrange("p j w -> p w j")
-            dst = g[:].rearrange("p (w j) -> p w j", j=4)
-            if eng == "v":
-                nc.vector.tensor_copy(out=dst, in_=src)
-            else:
-                nc.scalar.copy(out=dst, in_=src)
-            wgrp[i] = g
+            t = stage_tile("wg%d" % i)
+            copy_on(engine, t[:].rearrange("p (w j) -> p w j", j=PACK), w_raw.pop(i)[:].rearrange("p j w -> p w j"))
+            w_stage[i] = t
 
-        def w_quant(i):
-            if i >= NBLK * NPASS:
+        def w_quantize(i):
+            if i >= N_W:
                 return
-            c, g = i // NPASS, i % NPASS
-            wc[i] = ring.tile([P, NB], U32, name="wc%d" % i, tag="wc%d" % g, bufs=2, align_bytes=64)
+            block, g = i // N_PASSES, i % N_PASSES
+            w_codes[i] = ring.tile([P, COLS], U32, name="wc%d" % i, tag="wc%d" % g, bufs=2, align_bytes=64)
             if g % 4 == 0:
-                ws[(c, g // 4)] = ring.tile([P, NB], U8, name="ws%d_%d" % (c, g // 4), tag="ws%d" % (g // 4), bufs=2, align_bytes=64)
+                w_planes[(block, g // 4)] = ring.tile(
+                    [P, COLS], U8, name="ws%d_%d" % (block, g // 4), tag="ws%d" % (g // 4), bufs=2, align_bytes=64
+                )
             nc.vector.quantize_mx(
-                out=wc[i][:].bitcast(FP8X4),
-                scales=ws[(c, g // 4)][4 * (g % 4) : P, :],
-                in_=wgrp.pop(i)[:],
+                out=w_codes[i][:].bitcast(FP8X4),
+                scales=w_planes[(block, g // 4)][4 * (g % 4) : P, :],
+                in_=w_stage.pop(i)[:],
             )
+
 
         def beta_load():
-            t = ring.tile([P, N], BF16, name="braw", tag="kr", bufs=KR_BUFS)
+            t = ring.tile([P, N], BF16, name="braw", tag="kr", bufs=KEY_BUFS)
             nc.sync.dma_start(out=t[:], in_=beta.rearrange("b h n -> (b h) n"))
-            braw[0] = t
+            beta_raw[0] = t
 
-        def beta_turn(q):
-            bs = ring.tile([P, 512], F32, name="bs%d" % q, tag="tmp", bufs=3)
+        def beta_transpose(q):
+            by_t = ring.tile([P, K_PASS], F32, name="bs%d" % q, tag="tmp", bufs=DIFF_BUFS)
             nc.vector.tensor_copy(
-                out=bs[:].rearrange("r (t p) -> r t p", t=4),
-                in_=braw[0][:, 512 * q : 512 * (q + 1)].rearrange("r (p t) -> r t p", t=4),
+                out=by_t[:].rearrange("r (t p) -> r t p", t=PACK),
+                in_=beta_raw[0][:, K_PASS * q : K_PASS * (q + 1)].rearrange("r (p t) -> r t p", t=PACK),
             )
-            bank = psum.tile([P, 512], F32, name="bbk%d" % q, tag="ps", bufs=7)
-            for t in range(4):
-                nc.tensor.transpose(bank[:, P * t : P * (t + 1)], bs[:, P * t : P * (t + 1)], ident[:])
+            bank = psum.tile([P, 512], F32, name="bbk%d" % q, tag="ps", bufs=BANKS)
+            for t in range(PACK):
+                nc.tensor.transpose(bank[:, P * t : P * (t + 1)], by_t[:, P * t : P * (t + 1)], ident[:])
             nc.scalar.copy(
-                out=beta_t[:, 4 * q : 4 * q + 4, :],
-                in_=bank[:].rearrange("p (t r) -> p t r", t=4),
+                out=beta_t[:, PACK * q : PACK * (q + 1), :], in_=bank[:].rearrange("p (t r) -> p t r", t=PACK)
             )
 
-        def beta_block(c):
-            if c >= NBLK:
+        def beta_widen(block):
+            if block >= N_BLOCKS:
                 return
-            t = ring.tile([P, 16, B, HB], F32, name="bb%d" % c, tag="bb", bufs=2)
+            t = ring.tile([P, PACK * GROUPS_PER_BATCH, B, HEADS], F32, name="bb%d" % block, tag="bb", bufs=2)
             nc.gpsimd.tensor_copy(
                 out=t[:],
-                in_=beta_t[:].rearrange("p k (b h) -> p k b h", b=B)[:, :, :, HB * c : HB * (c + 1)],
+                in_=beta_t[:].rearrange("p k (b h) -> p k b h", b=B)[:, :, :, HEADS * block : HEADS * (block + 1)],
             )
-            bb[c] = t
+            beta_cols[block] = t
 
-        def v_load(u):
-            if u >= NUNIT:
+
+        def vo_load(u):
+            if u >= N_UNITS:
                 return
-            c, G = u // NG, u % NG
-            b, q = G // 4, G % 4
-            t = ring.tile([P, HB, 4 * DH], BF16, name="vt%d" % u, tag="vo", bufs=4)
+            block, group = u // N_GROUPS, u % N_GROUPS
+            b, q = group // GROUPS_PER_BATCH, group % GROUPS_PER_BATCH
+            t = ring.tile([P, HEADS, PACK * DH], BF16, name="vt%d" % u, tag="vo", bufs=VO_BUFS)
             nc.sync.dma_start(
                 out=t[:],
-                in_=vo[b, HB * c : HB * (c + 1), 512 * q : 512 * (q + 1), :].rearrange("h (p t) d -> p h (t d)", t=4),
+                in_=vo[b, HEADS * block : HEADS * (block + 1), K_PASS * q : K_PASS * (q + 1), :].rearrange(
+                    "h (p t) d -> p h (t d)", t=PACK
+                ),
             )
-            vt[u] = t
+            vo_dv[u] = t
 
-        def mm(u, t):
-            c, G = u // NG, u % NG
-            if c == 0:
-                x_need(4 * G + 1 + 2 * (t // 2))
-            if t % 2 == 0:
-                acc[(u, t // 2)] = psum.tile([P, 512], F32, name="acc%d_%d" % (u, t // 2), tag="ps", bufs=7)
-            bank = acc[(u, t // 2)]
-            for g in range(NPASS):
+        def multiply(u, t, passes):
+            block, group = u // N_GROUPS, u % N_GROUPS
+            if block == 0:
+                x_quantize_through(4 * group + 1 + 2 * (t // 2))
+            if t % 2 == 0 and passes[0] == 0:
+                v_bank[(u, t // 2)] = psum.tile([P, 512], F32, name="acc%d_%d" % (u, t // 2), tag="ps", bufs=BANKS)
+            for g in passes:
+                rows = slice(4 * (g % 4), P)
                 nc.tensor.matmul_mx(
-                    out=bank[:, NB * (t % 2) : NB * (t % 2 + 1)],
-                    lhsT=xc[(G, g // 2)][:, g % 2, P * t : P * (t + 1)].bitcast(FP8X4),
-                    lhsT_scale=xs[(G, g // 4)][4 * (g % 4) : P, P * t : P * (t + 1)],
-                    rhs=wc[c * NPASS + g][:].bitcast(FP8X4),
-                    rhs_scale=ws[(c, g // 4)][4 * (g % 4) : P, :],
+                    out=v_bank[(u, t // 2)][:, COLS * (t % 2) : COLS * (t % 2 + 1)],
+                    lhsT=x_codes[(group, g // 2)][:, g % 2, P * t : P * (t + 1)].bitcast(FP8X4),
+                    lhsT_scale=x_planes[(group, g // 4)][rows, P * t : P * (t + 1)],
+                    rhs=w_codes[block * N_PASSES + g][:].bitcast(FP8X4),
+                    rhs_scale=w_planes[(block, g // 4)][rows, :],
                     start=(g == 0),
-                    stop=(g == NPASS - 1),
+                    stop=(g == N_PASSES - 1),
                 )
 
-        def lift(u, hf):
-            if u < 0 or u >= NUNIT - 1:
+        def subtract_vo(u, i):
+            if u < 0 or u >= N_UNITS:
                 return
-            d = ring.tile([P, 512], F32, name="tmp%d_%d" % (u, hf), tag="tmp", bufs=3)
-            nc.scalar.copy(out=d[:], in_=acc.pop((u, hf))[:])
-            acc[(u, hf)] = d
-            tmp[(u, hf)] = d
-
-        def sub(u, hf):
-            if u < 0 or u >= NUNIT:
-                return
-            if (u, hf) in tmp:
-                d = tmp[(u, hf)]
-            else:
-                d = ring.tile([P, 512], F32, name="tmp%d_%d" % (u, hf), tag="tmp", bufs=3)
+            t = ring.tile([P, 512], F32, name="tmp%d_%d" % (u, i), tag="tmp", bufs=DIFF_BUFS)
             nc.vector.tensor_tensor(
-                out=d[:].rearrange("p (t h d) -> p t h d", t=2, h=HB),
-                in0=acc.pop((u, hf))[:].rearrange("p (t h d) -> p t h d", t=2, h=HB),
-                in1=vt[u][:].rearrange("p h (t d) -> p t h d", t=4)[:, 2 * hf : 2 * hf + 2],
+                out=t[:].rearrange("p (t h d) -> p t h d", t=2, h=HEADS),
+                in0=v_bank.pop((u, i))[:].rearrange("p (t h d) -> p t h d", t=2, h=HEADS),
+                in1=vo_dv[u][:].rearrange("p h (t d) -> p t h d", t=PACK)[:, 2 * i : 2 * i + 2],
                 op=ALU.subtract,
             )
-            tmp[(u, hf)] = d
+            diff[(u, i)] = t
 
-        def scale(u, hf):
-            if u < 0 or u >= NUNIT:
+        def times_beta(u, i):
+            if u < 0 or u >= N_UNITS:
                 return
-            c, G = u // NG, u % NG
-            b, q = G // 4, G % 4
-            d = tmp.pop((u, hf))
+            block, group = u // N_GROUPS, u % N_GROUPS
+            b, q = group // GROUPS_PER_BATCH, group % GROUPS_PER_BATCH
+            t_diff = diff.pop((u, i))
             for tl in range(2):
-                t = 2 * hf + tl
-                for h in range(HB):
+                t = 2 * i + tl
+                for h in range(HEADS):
                     nc.scalar.activation(
-                        out=vt[u][:, h, DH * t : DH * (t + 1)],
-                        in_=d[:, (tl * HB + h) * DH : (tl * HB + h + 1) * DH],
+                        out=vo_dv[u][:, h, DH * t : DH * (t + 1)],
+                        in_=t_diff[:, (tl * HEADS + h) * DH : (tl * HEADS + h + 1) * DH],
                         func=ACT.Copy,
-                        scale=bb[c][:, 4 * q + t, b, h : h + 1],
+                        scale=beta_cols[block][:, PACK * q + t, b, h : h + 1],
                     )
 
-        def dv_il(u, eng):
-            if u < 0 or u >= NUNIT:
+        def dv_interleave(u, engine):
+            if u < 0 or u >= N_UNITS:
                 return
-            g = ring.tile([P, 1024], BF16, name="dvg%d" % u, tag="g2", bufs=10, align_bytes=64)
-            src = vt.pop(u)[:].rearrange("p h (t d) -> p h d t", t=4)
-            dst = g[:].rearrange("p (h d t) -> p h d t", h=HB, t=4)
-            if eng == "v":
-                nc.vector.tensor_copy(out=dst, in_=src)
-            else:
-                nc.scalar.copy(out=dst, in_=src)
-            dvg[u] = g
+            t = stage_tile("dvg%d" % u)
+            copy_on(
+                engine,
+                t[:].rearrange("p (h d t) -> p h d t", h=HEADS, t=PACK),
+                vo_dv.pop(u)[:].rearrange("p h (t d) -> p h d t", t=PACK),
+            )
+            dv_stage[u] = t
 
-        def dv_quant(u):
-            if u < 0 or u >= NUNIT:
+        def dv_quantize(u):
+            if u < 0 or u >= N_UNITS:
                 return
-            q = u % 4
-            dvc[u] = ring.tile([P, NB], U32, name="dvc%d" % u, tag="dvc", bufs=8, align_bytes=64)
+            q = u % GROUPS_PER_BATCH
+            dv_codes[u] = ring.tile([P, COLS], U32, name="dvc%d" % u, tag="dvc", bufs=DV_BUFS, align_bytes=64)
             if q == 0:
-                dvs[u // 4] = ring.tile([P, NB], U8, name="dvs%d" % (u // 4), tag="dvs", bufs=2, align_bytes=64)
+                dv_planes[u // 4] = ring.tile([P, COLS], U8, name="dvs%d" % (u // 4), tag="dvs", bufs=2, align_bytes=64)
             nc.vector.quantize_mx(
-                out=dvc[u][:].bitcast(FP8X4),
-                scales=dvs[u // 4][4 * q : P, :],
-                in_=dvg.pop(u)[:],
+                out=dv_codes[u][:].bitcast(FP8X4), scales=dv_planes[u // 4][4 * q : P, :], in_=dv_stage.pop(u)[:]
             )
 
-        def head_of(i):
-            sg, hl = i // HB, i % HB
-            return sg % 2, HB * (sg // 2) + hl
 
-        def k_load(i):
-            if i < 0 or i >= NHEAD:
+        def key_load(i):
+            if i < 0 or i >= N_HEADS:
                 return
-            b, h = head_of(i)
-            t = ring.tile([P, 4, 512], BF16, name="kr%d" % i, tag="kr", bufs=KR_BUFS)
-            nc.sync.dma_start(out=t[:], in_=k_phi[b, h].rearrange("(q p t) s -> p q (t s)", q=4, t=4))
-            kraw[i] = t
+            b, h = (i // HEADS) % 2, HEADS * (i // HEADS // 2) + i % HEADS
+            t = ring.tile([P, GROUPS_PER_BATCH, K_PASS], BF16, name="kr%d" % i, tag="kr", bufs=KEY_BUFS)
+            nc.sync.dma_start(
+                out=t[:], in_=k_phi[b, h].rearrange("(q p t) s -> p q (t s)", q=GROUPS_PER_BATCH, t=PACK)
+            )
+            key_raw[i] = t
 
-        def k_il(i, hf, eng):
-            if i < 0 or i >= NHEAD or (i, hf) in kdone:
+        def key_interleave(i, half, engine):
+            if i < 0 or i >= N_HEADS:
                 return
-            kdone[(i, hf)] = 1
-            g = ring.tile([P, 1024], BF16, name="kg%d_%d" % (i, hf), tag="g2", bufs=10, align_bytes=64)
-            src = kraw[i][:, 2 * hf : 2 * hf + 2, :].rearrange("p q (t s) -> p q s t", t=4)
-            dst = g[:].rearrange("p (q s t) -> p q s t", q=2, t=4)
-            if eng == "v":
-                nc.vector.tensor_copy(out=dst, in_=src)
-            else:
-                nc.scalar.copy(out=dst, in_=src)
-            kgrp[(i, hf)] = g
+            t = stage_tile("kg%d_%d" % (i, half))
+            copy_on(
+                engine,
+                t[:].rearrange("p (q s t) -> p q s t", q=2, t=PACK),
+                key_raw[i][:, 2 * half : 2 * half + 2, :].rearrange("p q (t s) -> p q s t", t=PACK),
+            )
+            key_stage[(i, half)] = t
 
-        def k_quant(i, hf):
-            if i < 0 or i >= NHEAD or (i, hf) not in kgrp:
+        def key_quantize(i, half):
+            if i < 0 or i >= N_HEADS:
                 return
-            if hf == 0 and i < EARLY:
-                kc[i] = ring.tile([P, 512], U32, name="kc%d" % i, tag="kc", bufs=3, align_bytes=64)
-                ks[i] = ring.tile([P, 512], U8, name="ks%d" % i, tag="ks", bufs=3, align_bytes=64)
-            elif hf == 0:
-                if i == EARLY:
-                    ks["late"] = ring.tile([P, HB, 512], U8, name="kslate", tag="g2", bufs=10, align_bytes=64)
-                if i < NHEAD - 1:
-                    kc[i] = ring.tile([P, 512], U32, name="kc%d" % i, tag="wr", bufs=3, align_bytes=64)
+            if half == 0 and i < LAST_SET:
+                key_codes[i] = ring.tile([P, K_PASS], U32, name="kc%d" % i, tag="kc", bufs=CODE_BUFS, align_bytes=64)
+                key_planes[i] = ring.tile([P, K_PASS], U8, name="ks%d" % i, tag="ks", bufs=CODE_BUFS, align_bytes=64)
+            elif half == 0:
+                if i == LAST_SET:
+                    key_planes["last set"] = ring.tile(
+                        [P, HEADS, K_PASS], U8, name="kslate", tag="g2", bufs=STAGE_BUFS, align_bytes=64
+                    )
+                if i < N_HEADS - 1:
+                    key_codes[i] = ring.tile([P, K_PASS], U32, name="kc%d" % i, tag="wr", bufs=W_BUFS, align_bytes=64)
                 else:
-                    kc[i] = ring.tile([P, 512], U32, name="kc%d" % i, tag="g2", bufs=10, align_bytes=64)
-                ks[i] = ks["late"][:, i - EARLY, :]
-            cols = slice(256 * hf, 256 * (hf + 1))
+                    key_codes[i] = ring.tile([P, K_PASS], U32, name="kc%d" % i, tag="g2", bufs=STAGE_BUFS, align_bytes=64)
+                key_planes[i] = key_planes["last set"][:, i - LAST_SET, :]
+            cols = slice(256 * half, 256 * (half + 1))
             nc.vector.quantize_mx(
-                out=kc[i][:, cols].bitcast(FP8X4),
-                scales=ks[i][:, cols],
-                in_=kgrp.pop((i, hf))[:],
+                out=key_codes[i][:, cols].bitcast(FP8X4), scales=key_planes[i][:, cols], in_=key_stage.pop((i, half))[:]
             )
 
-        def s2(i):
-            if i < 0 or i >= NHEAD:
+        def second_stage(i):
+            if i < 0 or i >= N_HEADS:
                 return
-            sg, hl = i // HB, i % HB
-            if hl == 0 and i < EARLY:
-                o2[sg] = psum.tile([P, 512], F32, name="o2_%d" % sg, tag="o2", bufs=1)
-            elif hl == 0:
-                o2[sg] = psum.tile([P, 512], F32, name="o2_%d" % sg, tag="ps", bufs=7)
-            cols = slice(P * (hl // 2), P * (hl // 2 + 1))
-            for q in range(4):
+            st, h = i // HEADS, i % HEADS
+            if h == 0 and i < LAST_SET:
+                sums[st] = psum.tile([P, 512], F32, name="o2_%d" % st, tag="o2", bufs=1)
+            elif h == 0:
+                sums[st] = psum.tile([P, 512], F32, name="o2_%d" % st, tag="ps", bufs=BANKS)
+            cols = slice(P * (h // 2), P * (h // 2 + 1))
+            for q in range(GROUPS_PER_BATCH):
                 nc.tensor.matmul_mx(
-                    out=o2[sg][:, P * hl : P * (hl + 1)],
-                    lhsT=kc[i][:, P * q : P * (q + 1)].bitcast(FP8X4),
-                    lhsT_scale=ks[i][:, P * q : P * (q + 1)],
-                    rhs=dvc[4 * sg + q][:, cols].bitcast(FP8X4),
-                    rhs_scale=dvs[sg][4 * q : P, cols],
+                    out=sums[st][:, P * h : P * (h + 1)],
+                    lhsT=key_codes[i][:, P * q : P * (q + 1)].bitcast(FP8X4),
+                    lhsT_scale=key_planes[i][:, P * q : P * (q + 1)],
+                    rhs=dv_codes[4 * st + q][:, cols].bitcast(FP8X4),
+                    rhs_scale=dv_planes[st][4 * q : P, cols],
                     start=(q == 0),
-                    stop=(q == 3),
+                    stop=(q == GROUPS_PER_BATCH - 1),
                 )
 
-        def out_view(ap, sg):
-            b, c = sg % 2, sg // 2
-            return ap[b, HB * c : HB * (c + 1)].rearrange("h s d -> s h d")
+        def memory_view(ap, st):
+            b, block = st % 2, st // 2
+            return ap[b, HEADS * block : HEADS * (block + 1)].rearrange("h s d -> s h d")
 
-        def big_w_load(sg):
-            if sg < 0 or sg >= 2 * NBLK:
+        def memory_load(st):
+            if st < 0 or st >= N_SETS:
                 return
-            t = ring.tile([P, HB, DH], BF16, name="wt%d" % sg, tag="wt", bufs=2)
-            nc.sync.dma_start(out=t[:], in_=out_view(W, sg))
-            wt[sg] = t
+            t = ring.tile([P, HEADS, DH], BF16, name="wt%d" % st, tag="wt", bufs=2)
+            nc.sync.dma_start(out=t[:], in_=memory_view(W, st))
+            w_mem[st] = t
 
-        def evac(sg):
-            o = ring.tile([P, HB, DH], F32, name="osb%d" % sg, tag="osb", bufs=2)
+        def finish(st):
+            t = ring.tile([P, HEADS, DH], F32, name="osb%d" % st, tag="osb", bufs=2)
             nc.vector.tensor_tensor(
-                out=o[:].rearrange("p (j e) d -> p j e d", e=2),
-                in0=o2.pop(sg)[:].rearrange("p (j z d) -> p j z d", j=2, z=4)[:, :, 0:4:3, :],
-                in1=wt.pop(sg)[:].rearrange("p (j e) d -> p j e d", e=2),
+                out=t[:].rearrange("p (j e) d -> p j e d", e=2),
+                in0=sums.pop(st)[:].rearrange("p (j z d) -> p j z d", j=2, z=4)[:, :, 0:4:3, :],
+                in1=w_mem.pop(st)[:].rearrange("p (j e) d -> p j e d", e=2),
                 op=ALU.add,
             )
-            nc.sync.dma_start(out=out_view(out, sg), in_=o[:])
+            nc.sync.dma_start(out=memory_view(out, st), in_=t[:])
 
         x_load(0)
         x_load(1)
@@ -421,103 +417,94 @@ def tile_dpfpattention_pb_l_kernel(tc, x, wv, beta, vo, k_phi, W, out):
         x_load(5)
         for i in range(4, 7):
             w_load(i)
-        for n in range(6):
-            xq[x_tag(n)] = n
-        xq["next"] = 6
-        x_run(0)
-        x_copy(0, 0, "v")
-        for k in range(1, 4):
-            x_copy(0, k, "s")
-        for q in range(4):
-            beta_turn(q)
-        beta_block(0)
-        x_need(0)
-        x_run(1)
-        x_copy(1, 0, "v")
-        for k in range(1, 4):
-            x_copy(1, k, "s")
-        w_il(0, "v")
+        x_half_run(0, 0)
+        x_half_run(0, 1)
+        for q in range(GROUPS_PER_BATCH):
+            beta_transpose(q)
+        beta_widen(0)
+        x_half_run(1, 0)
+        x_half_run(1, 1)
+        w_interleave(0, "vector")
         w_load(7)
-        x_loads(1)
-        w_il(1, "v")
-        w_il(2, "s")
-        x_need(1)
-        w_quant(0)
-        w_quant(1)
-        w_il(3, "v")
-        w_quant(2)
-        x_turn(2)
-        w_il(4, "v")
-        w_il(5, "s")
-        w_quant(3)
-        w_quant(4)
-        w_il(6, "v")
-        w_quant(5)
-        w_il(7, "v")
-        w_quant(6)
+        x_load_ahead(1)
+        w_interleave(1, "vector")
+        w_interleave(2, "scalar")
+        x_quantize_through(1)
+        w_quantize(0)
+        w_quantize(1)
+        w_interleave(3, "vector")
+        w_quantize(2)
+        x_half_run(2, 0)
+        x_half_run(2, 1)
+        x_load_ahead(2)
+        w_interleave(4, "vector")
+        w_interleave(5, "scalar")
+        w_quantize(3)
+        w_quantize(4)
+        w_interleave(6, "vector")
+        w_quantize(5)
+        w_interleave(7, "vector")
+        w_quantize(6)
         w_load(8)
         w_load(9)
-        v_load(0)
-        v_load(1)
-        w_quant(7)
+        vo_load(0)
+        vo_load(1)
+        w_quantize(7)
 
-        for u in range(NSLICE):
-            v_load(u + 2)
+        for u in range(N_SLICES):
+            vo_load(u + 2)
             if u < 2:
                 w_load(u + 10)
             if u > 0:
                 w_load(u + 11)
-            if u >= NG and u + 2 - LAG_K < EARLY:
-                k_load(u + 2 - LAG_K)
-            if u == NG:
-                k_load(u + 1 - LAG_K)
-            if u < NG:
-                k_load(u + 1 - LAG_K)
-            if u >= LATE0 - 2 and (u - LATE0) % 2 == 0:
-                k_load(EARLY + (u - LATE0 + 2) // 2)
+            if u >= N_GROUPS and u + 2 - KEY_LAG < LAST_SET:
+                key_load(u + 2 - KEY_LAG)
+            if u <= N_GROUPS:
+                key_load(u + 1 - KEY_LAG)
+            if u >= IDLE_W - 2 and (u - IDLE_W) % 2 == 0:
+                key_load(LAST_SET + (u - IDLE_W + 2) // 2)
             if u % 4 == 2:
-                big_w_load((u - 2) // 4)
-            if u % NG == 4:
-                beta_block(u // NG + 1)
-            for j in range(4):
-                if j == 2 and u < NUNIT:
-                    s2(u - LAG_S2)
-                if j == 0 and u >= NUNIT:
-                    s2(u - LAG_S2)
-                if u < NUNIT:
-                    mm(u, j)
-                r = 4 * u + j + 3
-                if r < 32:
-                    x_turn(r)
+                memory_load((u - 2) // 4)
+            if u % N_GROUPS == 4:
+                beta_widen(u // N_GROUPS + 1)
+            head = u - KEY_LAG if u - KEY_LAG < LAST_SET else -1
+            early = u - IDLE_W
+            for j in range(PACK):
+                if j == (2 if u < N_UNITS else 0):
+                    second_stage(u - S2_LAG)
+                if 4 * u + j + RUN_LEAD < N_RUNS:
+                    for half in range(2):
+                        multiply(u, j, range(4 * half, 4 * half + 4))
+                        x_half_run(4 * u + j + RUN_LEAD, half)
+                    x_load_ahead(4 * u + j + RUN_LEAD)
+                elif u < N_UNITS:
+                    multiply(u, j, range(N_PASSES))
                 if j == 0:
-                    lift(u - 1, 1)
-                    if u > 0:
-                        w_il(u + 9, "s")
-                    if u == NUNIT:
-                        evac(2 * NBLK - 2)
-                    k_il(u - LAG_K, 0, "v")
-                    sub(u - 1, 1)
+                    subtract_vo(u - 1, 1)
+                    if u == N_UNITS:
+                        finish(N_SETS - 2)
+                    key_interleave(head, 0, "vector")
+                    times_beta(u - 1, 1)
                 elif j == 1:
                     if u > 0:
-                        w_quant(u + 8)
-                    if LATE0 < u <= LATE0 + 8:
-                        k_quant(EARLY + (u - LATE0 - 1) // 2, (u - LATE0 - 1) % 2)
-                    k_il(u - LAG_K, 1, "v")
-                    scale(u - 1, 1)
+                        w_quantize(u + 8)
+                    if 0 < early <= 8:
+                        key_quantize(LAST_SET + (early - 1) // 2, (early - 1) % 2)
+                    key_interleave(head, 1, "vector")
+                    dv_interleave(u - 1, "scalar" if u < N_UNITS else "vector")
                 elif j == 2:
-                    sub(u, 0)
-                    k_quant(u - LAG_K, 0)
-                    scale(u, 0)
-                    dv_il(u - 1, DV_IL[u % 2] if u < NUNIT else "v")
+                    subtract_vo(u, 0)
+                    key_quantize(head, 0)
+                    dv_quantize(u - 1)
+                    times_beta(u, 0)
                     if u == 0:
-                        w_il(8, "s")
+                        w_interleave(8, "scalar")
                 else:
                     if u == 0:
-                        w_quant(8)
-                        w_il(9, "s")
-                    k_quant(u - LAG_K, 1)
-                    dv_quant(u - 1)
-                    if u >= 8 and u % 4 == 0 and u != NUNIT:
-                        evac((u - 8) // 4)
-                    if LATE0 <= u < LATE0 + 8:
-                        k_il(EARLY + (u - LATE0) // 2, (u - LATE0) % 2, "s")
+                        w_quantize(8)
+                    key_quantize(head, 1)
+                    if u >= 8 and u % 4 == 0 and u != N_UNITS:
+                        finish((u - 8) // 4)
+                    w_interleave(u + 9, "scalar")
+                    if 0 <= early < 8:
+                        key_interleave(LAST_SET + early // 2, early % 2, "scalar")

from contextlib import ExitStack

import concourse.mybir as mybir
from concourse.masks import make_identity

F32 = mybir.dt.float32
BF16 = mybir.dt.bfloat16
U32 = mybir.dt.uint32
U8 = mybir.dt.uint8
FP8X4 = mybir.dt.float8_e4m3fn_x4
ALU = mybir.AluOpType
ACT = mybir.ActivationFunctionType

B, N, D, H, DH = 2, 2048, 4096, 64, 64
S = 2 * DH
FLOPS = 2 * B * N * D * H * DH + 2 * B * H * N * S * DH

P = 128
PACK = 4
K_PASS = P * PACK
COLS = 256
HEADS = COLS // DH
N_BLOCKS = H * DH // COLS
N_GROUPS = B * N // K_PASS
GROUPS_PER_BATCH = N // K_PASS
N_PASSES = D // K_PASS
N_UNITS = N_BLOCKS * N_GROUPS
N_SETS = B * N_BLOCKS
N_HEADS = B * H
N_W = N_BLOCKS * N_PASSES
N_PIECES = 8 * N_GROUPS
N_RUNS = N_PIECES // 2
QUANT = 1024

S2_LAG = 5
KEY_LAG = 4
N_SLICES = N_HEADS + S2_LAG + 1
RUN_LEAD = 3
LAST_SET = N_HEADS - HEADS
IDLE_W = N_UNITS - 9

KEY_BUFS = 5
W_BUFS = 3
VO_BUFS = 4
STAGE_BUFS = 10
DIFF_BUFS = 3
DV_BUFS = 8
CODE_BUFS = 3
BANKS = 7


def tile_dpfpattention_pb_l_kernel(tc, x, wv, beta, vo, k_phi, W, out):
    nc = tc.nc
    with ExitStack() as ctx:
        keep = ctx.enter_context(tc.tile_pool(name="keep", bufs=1))
        ring = ctx.enter_context(tc.tile_pool(name="ring", bufs=2))
        psum = ctx.enter_context(tc.psum_pool(name="psum", bufs=1))
        ctx.enter_context(tc.manual_schedule())

        x_view = x.flatten_outer_dims().rearrange("(g m t) k -> g m t k", m=P, t=PACK)

        ident = keep.tile([P, P], F32, name="ident", tag="ident")
        make_identity(nc, ident[:])
        beta_t = keep.tile([P, PACK * GROUPS_PER_BATCH, N_HEADS], BF16, name="beta_t", tag="beta_t")

        x_raw, x_bank, x_stage, x_codes, x_planes = {}, {}, {}, {}, {}
        w_raw, w_stage, w_codes, w_planes = {}, {}, {}, {}
        key_raw, key_stage, key_codes, key_planes = {}, {}, {}, {}
        vo_dv, v_bank, diff, dv_stage, dv_codes, dv_planes = {}, {}, {}, {}, {}, {}
        beta_raw, beta_cols, sums, w_mem = {}, {}, {}, {}
        x_state = {"next piece": 0, "quantised run": -1}

        def copy_on(engine, dst, src):
            if engine == "vector":
                nc.vector.tensor_copy(out=dst, in_=src)
            else:
                nc.scalar.copy(out=dst, in_=src)

        def stage_tile(name):
            return ring.tile([P, QUANT], BF16, name=name, tag="g2", bufs=STAGE_BUFS, align_bytes=64)


        def x_raw_tag(n):
            group = n // 8
            if group <= 5:
                return "xc%d_%d" % (6 + (n % 8) // 4, n % 4)
            if group == 6 and n % 2 == 0:
                return "xc7_%d" % ((n // 2) % 4)
            return "kr"

        def x_load(n):
            group, tp, kq = n // 8, (n % 8) // 4, n % 4
            tag = x_raw_tag(n)
            if tag == "kr":
                t = ring.tile([P, 2, 1024], BF16, name="xr%d" % n, tag="kr", bufs=KEY_BUFS)
            else:
                t = keep.tile([P, 2, 1024], BF16, name="xr%d" % n, tag=tag, align_bytes=64)
            nc.sync.dma_start(out=t[:], in_=x_view[group, :, 2 * tp : 2 * tp + 2, 1024 * kq : 1024 * (kq + 1)])
            x_raw[n] = t
            x_state[tag] = n
            x_state["next piece"] = n + 1

        def x_load_ahead(turned):
            while x_state["next piece"] < N_PIECES:
                n = x_state["next piece"]
                tag = x_raw_tag(n)
                if n // 2 > turned + 4:
                    return
                if tag == "kr":
                    if len([m for m in range(2 * turned + 2, n) if x_raw_tag(m) == "kr"]) >= 3:
                        return
                elif x_state.get(tag, -2) // 2 > turned:
                    return
                x_load(n)

        def x_transpose(r, half):
            for i in (2 * half, 2 * half + 1):
                words = x_raw[2 * r + i // 2][:].bitcast(F32)
                first = 256 * (i % 2)
                bank = psum.tile([P, 512], F32, name="xb%d_%d" % (r, i), tag="ps", bufs=BANKS)
                for tt in range(2):
                    for u in range(2):
                        nc.tensor.transpose(
                            bank[:, (2 * tt + u) * P : (2 * tt + u + 1) * P],
                            words[:, tt, first + u : first + 256 : 2],
                            ident[:],
                        )
                x_bank[(r, i)] = bank

        def x_copy(r, i, engine):
            t = stage_tile("xg%d_%d" % (r, i))
            copy_on(
                engine,
                t[:].bitcast(F32).rearrange("p (tt m u) -> p tt m u", tt=2, u=2),
                x_bank.pop((r, i))[:].rearrange("p (tt u m) -> p tt m u", tt=2, u=2),
            )
            x_stage[(r, i)] = t

        def x_quantize(r, i):
            n = 2 * r + i // 2
            group, tp, kq = n // 8, (n % 8) // 4, n % 4
            g = 2 * kq + i % 2
            if (group, kq) not in x_codes:
                x_codes[(group, kq)] = keep.tile(
                    [P, 2, K_PASS], U32, name="xc%d_%d" % (group, kq), tag="xc%d_%d" % (group, kq), align_bytes=64
                )
            if (group, g // 4) not in x_planes:
                x_planes[(group, g // 4)] = keep.tile(
                    [P, K_PASS], U8, name="xs%d_%d" % (group, g // 4), tag="xs%d_%d" % (group, g // 4), align_bytes=64
                )
            cols = slice(256 * tp, 256 * (tp + 1))
            nc.vector.quantize_mx(
                out=x_codes[(group, kq)][:, g % 2, cols].bitcast(FP8X4),
                scales=x_planes[(group, g // 4)][4 * (g % 4) : P, cols],
                in_=x_stage.pop((r, i))[:],
            )

        def x_quantize_through(r):
            while x_state["quantised run"] < r:
                x_state["quantised run"] += 1
                for i in range(4):
                    x_quantize(x_state["quantised run"], i)

        def x_half_run(r, half):
            x_transpose(r, half)
            if half == 0:
                x_quantize_through(r - 1)
                x_copy(r, 0, "vector")
                x_copy(r, 1, "scalar")
            else:
                x_copy(r, 2, "scalar")
                x_copy(r, 3, "scalar")


        def w_load(i):
            if i >= N_W:
                return
            block, g = i // N_PASSES, i % N_PASSES
            if 3 <= i <= 6:
                t = ring.tile([P, PACK, COLS], BF16, name="wr%d" % i, tag="vo", bufs=VO_BUFS)
            else:
                t = ring.tile([P, PACK, COLS], BF16, name="wr%d" % i, tag="wr", bufs=W_BUFS, align_bytes=64)
            nc.sync.dma_start(
                out=t[:],
                in_=wv[K_PASS * g : K_PASS * (g + 1), COLS * block : COLS * (block + 1)].rearrange(
                    "(p j) w -> p j w", j=PACK
                ),
            )
            w_raw[i] = t

        def w_interleave(i, engine):
            if i >= N_W:
                return
            t = stage_tile("wg%d" % i)
            copy_on(engine, t[:].rearrange("p (w j) -> p w j", j=PACK), w_raw.pop(i)[:].rearrange("p j w -> p w j"))
            w_stage[i] = t

        def w_quantize(i):
            if i >= N_W:
                return
            block, g = i // N_PASSES, i % N_PASSES
            w_codes[i] = ring.tile([P, COLS], U32, name="wc%d" % i, tag="wc%d" % g, bufs=2, align_bytes=64)
            if g % 4 == 0:
                w_planes[(block, g // 4)] = ring.tile(
                    [P, COLS], U8, name="ws%d_%d" % (block, g // 4), tag="ws%d" % (g // 4), bufs=2, align_bytes=64
                )
            nc.vector.quantize_mx(
                out=w_codes[i][:].bitcast(FP8X4),
                scales=w_planes[(block, g // 4)][4 * (g % 4) : P, :],
                in_=w_stage.pop(i)[:],
            )


        def beta_load():
            t = ring.tile([P, N], BF16, name="braw", tag="kr", bufs=KEY_BUFS)
            nc.sync.dma_start(out=t[:], in_=beta.rearrange("b h n -> (b h) n"))
            beta_raw[0] = t

        def beta_transpose(q):
            by_t = ring.tile([P, K_PASS], F32, name="bs%d" % q, tag="tmp", bufs=DIFF_BUFS)
            nc.vector.tensor_copy(
                out=by_t[:].rearrange("r (t p) -> r t p", t=PACK),
                in_=beta_raw[0][:, K_PASS * q : K_PASS * (q + 1)].rearrange("r (p t) -> r t p", t=PACK),
            )
            bank = psum.tile([P, 512], F32, name="bbk%d" % q, tag="ps", bufs=BANKS)
            for t in range(PACK):
                nc.tensor.transpose(bank[:, P * t : P * (t + 1)], by_t[:, P * t : P * (t + 1)], ident[:])
            nc.scalar.copy(
                out=beta_t[:, PACK * q : PACK * (q + 1), :], in_=bank[:].rearrange("p (t r) -> p t r", t=PACK)
            )

        def beta_widen(block):
            if block >= N_BLOCKS:
                return
            t = ring.tile([P, PACK * GROUPS_PER_BATCH, B, HEADS], F32, name="bb%d" % block, tag="bb", bufs=2)
            nc.gpsimd.tensor_copy(
                out=t[:],
                in_=beta_t[:].rearrange("p k (b h) -> p k b h", b=B)[:, :, :, HEADS * block : HEADS * (block + 1)],
            )
            beta_cols[block] = t


        def vo_load(u):
            if u >= N_UNITS:
                return
            block, group = u // N_GROUPS, u % N_GROUPS
            b, q = group // GROUPS_PER_BATCH, group % GROUPS_PER_BATCH
            t = ring.tile([P, HEADS, PACK * DH], BF16, name="vt%d" % u, tag="vo", bufs=VO_BUFS)
            nc.sync.dma_start(
                out=t[:],
                in_=vo[b, HEADS * block : HEADS * (block + 1), K_PASS * q : K_PASS * (q + 1), :].rearrange(
                    "h (p t) d -> p h (t d)", t=PACK
                ),
            )
            vo_dv[u] = t

        def multiply(u, t, passes):
            block, group = u // N_GROUPS, u % N_GROUPS
            if block == 0:
                x_quantize_through(4 * group + 1 + 2 * (t // 2))
            if t % 2 == 0 and passes[0] == 0:
                v_bank[(u, t // 2)] = psum.tile([P, 512], F32, name="acc%d_%d" % (u, t // 2), tag="ps", bufs=BANKS)
            for g in passes:
                rows = slice(4 * (g % 4), P)
                nc.tensor.matmul_mx(
                    out=v_bank[(u, t // 2)][:, COLS * (t % 2) : COLS * (t % 2 + 1)],
                    lhsT=x_codes[(group, g // 2)][:, g % 2, P * t : P * (t + 1)].bitcast(FP8X4),
                    lhsT_scale=x_planes[(group, g // 4)][rows, P * t : P * (t + 1)],
                    rhs=w_codes[block * N_PASSES + g][:].bitcast(FP8X4),
                    rhs_scale=w_planes[(block, g // 4)][rows, :],
                    start=(g == 0),
                    stop=(g == N_PASSES - 1),
                )

        def subtract_vo(u, i):
            if u < 0 or u >= N_UNITS:
                return
            t = ring.tile([P, 512], F32, name="tmp%d_%d" % (u, i), tag="tmp", bufs=DIFF_BUFS)
            nc.vector.tensor_tensor(
                out=t[:].rearrange("p (t h d) -> p t h d", t=2, h=HEADS),
                in0=v_bank.pop((u, i))[:].rearrange("p (t h d) -> p t h d", t=2, h=HEADS),
                in1=vo_dv[u][:].rearrange("p h (t d) -> p t h d", t=PACK)[:, 2 * i : 2 * i + 2],
                op=ALU.subtract,
            )
            diff[(u, i)] = t

        def times_beta(u, i):
            if u < 0 or u >= N_UNITS:
                return
            block, group = u // N_GROUPS, u % N_GROUPS
            b, q = group // GROUPS_PER_BATCH, group % GROUPS_PER_BATCH
            t_diff = diff.pop((u, i))
            for tl in range(2):
                t = 2 * i + tl
                for h in range(HEADS):
                    nc.scalar.activation(
                        out=vo_dv[u][:, h, DH * t : DH * (t + 1)],
                        in_=t_diff[:, (tl * HEADS + h) * DH : (tl * HEADS + h + 1) * DH],
                        func=ACT.Copy,
                        scale=beta_cols[block][:, PACK * q + t, b, h : h + 1],
                    )

        def dv_interleave(u, engine):
            if u < 0 or u >= N_UNITS:
                return
            t = stage_tile("dvg%d" % u)
            copy_on(
                engine,
                t[:].rearrange("p (h d t) -> p h d t", h=HEADS, t=PACK),
                vo_dv.pop(u)[:].rearrange("p h (t d) -> p h d t", t=PACK),
            )
            dv_stage[u] = t

        def dv_quantize(u):
            if u < 0 or u >= N_UNITS:
                return
            q = u % GROUPS_PER_BATCH
            dv_codes[u] = ring.tile([P, COLS], U32, name="dvc%d" % u, tag="dvc", bufs=DV_BUFS, align_bytes=64)
            if q == 0:
                dv_planes[u // 4] = ring.tile([P, COLS], U8, name="dvs%d" % (u // 4), tag="dvs", bufs=2, align_bytes=64)
            nc.vector.quantize_mx(
                out=dv_codes[u][:].bitcast(FP8X4), scales=dv_planes[u // 4][4 * q : P, :], in_=dv_stage.pop(u)[:]
            )


        def key_load(i):
            if i < 0 or i >= N_HEADS:
                return
            b, h = (i // HEADS) % 2, HEADS * (i // HEADS // 2) + i % HEADS
            t = ring.tile([P, GROUPS_PER_BATCH, K_PASS], BF16, name="kr%d" % i, tag="kr", bufs=KEY_BUFS)
            nc.sync.dma_start(
                out=t[:], in_=k_phi[b, h].rearrange("(q p t) s -> p q (t s)", q=GROUPS_PER_BATCH, t=PACK)
            )
            key_raw[i] = t

        def key_interleave(i, half, engine):
            if i < 0 or i >= N_HEADS:
                return
            t = stage_tile("kg%d_%d" % (i, half))
            copy_on(
                engine,
                t[:].rearrange("p (q s t) -> p q s t", q=2, t=PACK),
                key_raw[i][:, 2 * half : 2 * half + 2, :].rearrange("p q (t s) -> p q s t", t=PACK),
            )
            key_stage[(i, half)] = t

        def key_quantize(i, half):
            if i < 0 or i >= N_HEADS:
                return
            if half == 0 and i < LAST_SET:
                key_codes[i] = ring.tile([P, K_PASS], U32, name="kc%d" % i, tag="kc", bufs=CODE_BUFS, align_bytes=64)
                key_planes[i] = ring.tile([P, K_PASS], U8, name="ks%d" % i, tag="ks", bufs=CODE_BUFS, align_bytes=64)
            elif half == 0:
                if i == LAST_SET:
                    key_planes["last set"] = ring.tile(
                        [P, HEADS, K_PASS], U8, name="kslate", tag="g2", bufs=STAGE_BUFS, align_bytes=64
                    )
                if i < N_HEADS - 1:
                    key_codes[i] = ring.tile([P, K_PASS], U32, name="kc%d" % i, tag="wr", bufs=W_BUFS, align_bytes=64)
                else:
                    key_codes[i] = ring.tile([P, K_PASS], U32, name="kc%d" % i, tag="g2", bufs=STAGE_BUFS, align_bytes=64)
                key_planes[i] = key_planes["last set"][:, i - LAST_SET, :]
            cols = slice(256 * half, 256 * (half + 1))
            nc.vector.quantize_mx(
                out=key_codes[i][:, cols].bitcast(FP8X4), scales=key_planes[i][:, cols], in_=key_stage.pop((i, half))[:]
            )

        def second_stage(i):
            if i < 0 or i >= N_HEADS:
                return
            st, h = i // HEADS, i % HEADS
            if h == 0 and i < LAST_SET:
                sums[st] = psum.tile([P, 512], F32, name="o2_%d" % st, tag="o2", bufs=1)
            elif h == 0:
                sums[st] = psum.tile([P, 512], F32, name="o2_%d" % st, tag="ps", bufs=BANKS)
            cols = slice(P * (h // 2), P * (h // 2 + 1))
            for q in range(GROUPS_PER_BATCH):
                nc.tensor.matmul_mx(
                    out=sums[st][:, P * h : P * (h + 1)],
                    lhsT=key_codes[i][:, P * q : P * (q + 1)].bitcast(FP8X4),
                    lhsT_scale=key_planes[i][:, P * q : P * (q + 1)],
                    rhs=dv_codes[4 * st + q][:, cols].bitcast(FP8X4),
                    rhs_scale=dv_planes[st][4 * q : P, cols],
                    start=(q == 0),
                    stop=(q == GROUPS_PER_BATCH - 1),
                )

        def memory_view(ap, st):
            b, block = st % 2, st // 2
            return ap[b, HEADS * block : HEADS * (block + 1)].rearrange("h s d -> s h d")

        def memory_load(st):
            if st < 0 or st >= N_SETS:
                return
            t = ring.tile([P, HEADS, DH], BF16, name="wt%d" % st, tag="wt", bufs=2)
            nc.sync.dma_start(out=t[:], in_=memory_view(W, st))
            w_mem[st] = t

        def finish(st):
            t = ring.tile([P, HEADS, DH], F32, name="osb%d" % st, tag="osb", bufs=2)
            nc.vector.tensor_tensor(
                out=t[:].rearrange("p (j e) d -> p j e d", e=2),
                in0=sums.pop(st)[:].rearrange("p (j z d) -> p j z d", j=2, z=4)[:, :, 0:4:3, :],
                in1=w_mem.pop(st)[:].rearrange("p (j e) d -> p j e d", e=2),
                op=ALU.add,
            )
            nc.sync.dma_start(out=memory_view(out, st), in_=t[:])

        x_load(0)
        x_load(1)
        beta_load()
        x_load(2)
        x_load(3)
        for i in range(4):
            w_load(i)
        x_load(4)
        x_load(5)
        for i in range(4, 7):
            w_load(i)
        x_half_run(0, 0)
        x_half_run(0, 1)
        for q in range(GROUPS_PER_BATCH):
            beta_transpose(q)
        beta_widen(0)
        x_half_run(1, 0)
        x_half_run(1, 1)
        w_interleave(0, "vector")
        w_load(7)
        x_load_ahead(1)
        w_interleave(1, "vector")
        w_interleave(2, "scalar")
        x_quantize_through(1)
        w_quantize(0)
        w_quantize(1)
        w_interleave(3, "vector")
        w_quantize(2)
        x_half_run(2, 0)
        x_half_run(2, 1)
        x_load_ahead(2)
        w_interleave(4, "vector")
        w_interleave(5, "scalar")
        w_quantize(3)
        w_quantize(4)
        w_interleave(6, "vector")
        w_quantize(5)
        w_interleave(7, "vector")
        w_quantize(6)
        w_load(8)
        w_load(9)
        vo_load(0)
        vo_load(1)
        w_quantize(7)

        for u in range(N_SLICES):
            vo_load(u + 2)
            if u < 2:
                w_load(u + 10)
            if u > 0:
                w_load(u + 11)
            if u >= N_GROUPS and u + 2 - KEY_LAG < LAST_SET:
                key_load(u + 2 - KEY_LAG)
            if u <= N_GROUPS:
                key_load(u + 1 - KEY_LAG)
            if u >= IDLE_W - 2 and (u - IDLE_W) % 2 == 0:
                key_load(LAST_SET + (u - IDLE_W + 2) // 2)
            if u % 4 == 2:
                memory_load((u - 2) // 4)
            if u % N_GROUPS == 4:
                beta_widen(u // N_GROUPS + 1)
            head = u - KEY_LAG if u - KEY_LAG < LAST_SET else -1
            early = u - IDLE_W
            for j in range(PACK):
                if j == (2 if u < N_UNITS else 0):
                    second_stage(u - S2_LAG)
                if 4 * u + j + RUN_LEAD < N_RUNS:
                    for half in range(2):
                        multiply(u, j, range(4 * half, 4 * half + 4))
                        x_half_run(4 * u + j + RUN_LEAD, half)
                    x_load_ahead(4 * u + j + RUN_LEAD)
                elif u < N_UNITS:
                    multiply(u, j, range(N_PASSES))
                if j == 0:
                    subtract_vo(u - 1, 1)
                    if u == N_UNITS:
                        finish(N_SETS - 2)
                    key_interleave(head, 0, "vector")
                    times_beta(u - 1, 1)
                elif j == 1:
                    if u > 0:
                        w_quantize(u + 8)
                    if 0 < early <= 8:
                        key_quantize(LAST_SET + (early - 1) // 2, (early - 1) % 2)
                    key_interleave(head, 1, "vector")
                    dv_interleave(u - 1, "scalar" if u < N_UNITS else "vector")
                elif j == 2:
                    subtract_vo(u, 0)
                    key_quantize(head, 0)
                    dv_quantize(u - 1)
                    times_beta(u, 0)
                    if u == 0:
                        w_interleave(8, "scalar")
                else:
                    if u == 0:
                        w_quantize(8)
                    key_quantize(head, 1)
                    if u >= 8 and u % 4 == 0 and u != N_UNITS:
                        finish((u - 8) // 4)
                    w_interleave(u + 9, "scalar")
                    if 0 <= early < 8:
                        key_interleave(LAST_SET + early // 2, early % 2, "scalar")
